import numpy as np
import ml_dtypes


def mxq(x, axis, fmt="e4m3"):
    dtype, down = {"e4m3": (ml_dtypes.float8_e4m3fn, 7), "e5m2": (ml_dtypes.float8_e5m2, 14)}[fmt]
    v = np.moveaxis(np.asarray(x, np.float32).astype(ml_dtypes.bfloat16).astype(np.float64), axis, -1)
    blocks = v.reshape(v.shape[:-1] + (-1, 32))
    amax = np.abs(blocks).max(-1, keepdims=True)
    byte = np.maximum(np.where(amax > 0, np.frexp(amax)[1] - 1 + 127, 0) - down, 1)
    scale = np.exp2(byte - 127.0)
    codes = (blocks / scale).astype(np.float32).astype(dtype).astype(np.float64)
    return np.moveaxis((codes * scale).reshape(v.shape), -1, axis)


WIDE = False


def mx_kscale(k):
    if not WIDE:
        return np.ones(k)
    levels = np.array([10, -10, 5, -5, 0])
    if k % 512:
        return np.exp2(np.random.permutation(np.resize(levels, k // 32))).repeat(32)
    a = np.empty((k // 512, 16))
    for p in range(k // 512):
        a[p, :8] = np.random.permutation(np.resize(levels, 8))
        for g in range(8):
            far = levels[np.abs(levels - a[p, g]) >= 10]
            a[p, g + 8] = far[np.random.randint(len(far))]
    return np.exp2(a.ravel()).repeat(32)


BF16 = ml_dtypes.bfloat16


def bf(x):
    return np.asarray(x, np.float32).astype(BF16)


def f64(x):
    return np.asarray(x).astype(np.float64)


B, S, IN, OUT, R, RT = 4, 2048, 1024, 512, 512, 64


def setup_inputs():
    r, t = mx_kscale(R), mx_kscale(IN)
    return {
        "x": bf(np.random.standard_normal((B, S, IN)) * t),
        "siva_u_t": bf(np.random.standard_normal((OUT, RT)) * 1.7 / np.sqrt(R) * r[:RT]),
        "siva_u_d": bf(np.random.standard_normal((OUT, R - RT)) * 1.7 / np.sqrt(R) * r[RT:]),
        "siva_s": bf(np.random.uniform(0.0, 1.0, R)),
        "siva_v_t": bf(np.random.standard_normal((RT, IN)) / np.sqrt(IN) / r[:RT, None] / t),
        "siva_v_d": bf(np.random.standard_normal((R - RT, IN)) / np.sqrt(IN) / r[RT:, None] / t),
        "bias": bf(np.random.standard_normal(OUT) * 0.5),
    }


def reference(x, siva_u_t, siva_u_d, siva_s, siva_v_t, siva_v_d, bias):
    siva_u = np.concatenate((f64(siva_u_t), f64(siva_u_d)), axis=1)
    siva_v = np.concatenate((f64(siva_v_t), f64(siva_v_d)), axis=0)
    weight = mxq(siva_u * f64(siva_s), 1, "e4m3") @ mxq(siva_v, 0, "e4m3")
    return (mxq(f64(x), 2, "e4m3") @ mxq(weight, 1, "e4m3").T) + f64(bias)

@@ -1,0 +1,245 @@
+from contextlib import ExitStack
+
+import concourse.masks as masks
+import concourse.mybir as mybir
+
+BF16 = mybir.dt.bfloat16
+F32 = mybir.dt.float32
+I32 = mybir.dt.int32
+U32 = mybir.dt.uint32
+U8 = mybir.dt.uint8
+FP8X4 = mybir.dt.float8_e4m3fn_x4
+ADD = mybir.AluOpType.add
+MULT = mybir.AluOpType.mult
+
+P = 128
+TOKENS = 8192
+IN = 1024
+OUT = 512
+R = 512
+RT = 64
+SLOTS = 4
+GROUPS = TOKENS // (P * SLOTS)
+FLOPS = 2 * OUT * R * IN + 2 * TOKENS * IN * OUT
+
+RX = 10
+NG = 3
+NC = 4
+NO = 4
+FINE = 13
+
+
+def tile_sivalinear_t_kernel(
+    tc, x, siva_u_t, siva_u_d, siva_s, siva_v_t, siva_v_d, bias, out
+):
+    nc = tc.nc
+    xg = x.flatten_outer_dims().rearrange("(i p s) k -> i p (s k)", p=P, s=SLOTS)
+    og = out.flatten_outer_dims().rearrange("(i p s) n -> i p (s n)", p=P, s=SLOTS)
+
+    with ExitStack() as ctx:
+        const = ctx.enter_context(tc.tile_pool(name="const", bufs=1))
+        xpool = ctx.enter_context(tc.tile_pool(name="xpool", bufs=1))
+        gpool = ctx.enter_context(tc.tile_pool(name="gpool", bufs=1))
+        cpool = ctx.enter_context(tc.tile_pool(name="cpool", bufs=1))
+        opool = ctx.enter_context(tc.tile_pool(name="opool", bufs=1))
+        psum = ctx.enter_context(tc.psum_pool(name="psum", bufs=1))
+        ctx.enter_context(tc.manual_schedule())
+
+        rows = const.tile([P, OUT], BF16, name="rows")
+        ones = const.tile([P, P], BF16, name="ones")
+        ident_f = const.tile([P, P], F32, name="ident_f")
+        nc.vector.memset(rows[:].bitcast(I32), 0)
+        nc.vector.memset(ones[:], 1.0)
+        masks.make_identity(nc, ident_f[:])
+
+        s_col = const.tile([P, 4], BF16, name="s_col")
+        u_sb = const.tile([P, 4 * R], BF16, name="u_sb")
+        v_sb = const.tile([P, 4, IN], BF16, name="v_sb")
+        u3 = u_sb[:].rearrange("p (o r) -> p o r", o=4)
+        nc.sync.dma_start(
+            out=s_col[:],
+            in_=siva_s.rearrange("(q j) -> q j", j=4),
+        )
+        nc.sync.dma_start(out=u3[:, :, RT:R], in_=siva_u_d.rearrange("(o p) r -> p o r", p=P))
+        nc.sync.dma_start(out=u3[:, :, 0:RT], in_=siva_u_t.rearrange("(o p) r -> p o r", p=P))
+        nc.scalar.dma_start(out=rows[0:1, :], in_=bias.rearrange("(o n) -> o n", o=1))
+        qt = RT // 4
+        nc.sync.dma_start(out=v_sb[qt:P, :, :], in_=siva_v_d.rearrange("(q j) c -> q j c", j=4))
+        nc.sync.dma_start(out=v_sb[0:qt, :, :], in_=siva_v_t.rearrange("(q j) c -> q j c", j=4))
+
+        xs = {}
+
+        def load_x(i, pieces):
+            t = xpool.tile([P, SLOTS * IN], BF16, name="xs", tag="xs%d" % (i % RX))
+            w = SLOTS * IN // pieces
+            for h in range(pieces):
+                nc.sync.dma_start(out=t[:, h * w : (h + 1) * w], in_=xg[i][:, h * w : (h + 1) * w])
+            xs[i] = t
+
+        load_x(0, 2)
+        for i in range(1, RX):
+            load_x(i, 1)
+
+        gu = const.tile([P, OUT, 4], BF16, name="gu", align_bytes=64)
+        uw = u_sb[:].bitcast(F32)
+        s_b = s_col[:].rearrange("q (a e) -> q a e", a=2).unsqueeze(1).to_broadcast([P, P, 2, 2])
+        utbs = []
+        for b in range(2):
+            utb = psum.tile([P, 4 * P], F32, name="utb", tag="acc%d" % b)
+            for k in range(4):
+                w0 = (2 * b + k // 2) * 256
+                nc.tensor.transpose(utb[:, k * P : (k + 1) * P], uw[:, w0 + k % 2 : w0 + 256 : 2], ident_f[:])
+            utbs.append(utb)
+
+        ps_b = psum.tile([P, OUT], F32, name="ps_b", tag="acc2")
+        nc.tensor.matmul(out=ps_b[:], lhsT=ones[:], rhs=rows[:], start=True, stop=True)
+        bias_bc = const.tile([P, OUT], F32, name="bias_bc")
+        nc.scalar.copy(out=bias_bc[:], in_=ps_b[:])
+
+        for o in range(4):
+            u16 = utbs[o // 2][:].bitcast(BF16).rearrange(
+                "p (o a n e) -> p o a n e", o=2, a=2, n=P, e=2
+            )
+            nc.vector.tensor_tensor(
+                out=gu[:, o * P : (o + 1) * P, :].rearrange("p n (a e) -> p n a e", a=2),
+                in0=u16[:, o % 2].rearrange("p a n e -> p n a e"),
+                in1=s_b,
+                op=MULT,
+            )
+
+        gv = const.tile([P, IN, 4], BF16, name="gv", align_bytes=64)
+
+        def regroup_v(a, eng_copy):
+            eng_copy(
+                out=gv[:, a * 256 : (a + 1) * 256, :].rearrange("q (e p) j -> q e p j", e=2),
+                in_=v_sb[:, :, a // 2 * 512 : (a // 2 + 1) * 512].rearrange("q j (p t) -> q t p j", t=4)[
+                    :, a % 2 * 2 : a % 2 * 2 + 2
+                ],
+            )
+
+        u_codes = const.tile([P, OUT], U32, name="u_codes", align_bytes=64)
+        u_scales = const.tile([P, OUT], U8, name="u_scales", align_bytes=64)
+        v_codes = const.tile([P, IN], U32, name="v_codes", align_bytes=64)
+        v_scales = const.tile([P, IN], U8, name="v_scales", align_bytes=64)
+
+        def quant_v(g):
+            nc.vector.quantize_mx(
+                out=v_codes[:, g * 512 : (g + 1) * 512].bitcast(FP8X4),
+                scales=v_scales[:, g * 512 : (g + 1) * 512],
+                in_=gv[:, g * 512 : (g + 1) * 512, :].rearrange("q c j -> q (c j)"),
+            )
+
+        regroup_v(2, nc.scalar.copy)
+        regroup_v(3, nc.scalar.copy)
+        regroup_v(0, nc.vector.tensor_copy)
+        regroup_v(1, nc.vector.tensor_copy)
+        nc.vector.quantize_mx(
+            out=u_codes[:].bitcast(FP8X4),
+            scales=u_scales[:],
+            in_=gu[:].rearrange("p n t -> p (n t)"),
+        )
+        quant_v(0)
+        quant_v(1)
+
+        gw = const.tile([P, 2, OUT, 4], BF16, name="gw", align_bytes=64)
+        w_codes = const.tile([P, 2 * OUT], U32, name="w_codes", align_bytes=64)
+        w_scales = const.tile([P, 2 * OUT], U8, name="w_scales", align_bytes=64)
+
+        def weight_half(g):
+            for c in range(4):
+                wt = psum.tile([P, 4, P], F32, name="wt", tag="acc%d" % c)
+                for t in range(4):
+                    m = (4 * g + t) * P
+                    nc.tensor.matmul_mx(
+                        out=wt[:, t, :],
+                        lhsT=v_codes[:, m : m + P].bitcast(FP8X4),
+                        lhsT_scale=v_scales[:, m : m + P],
+                        rhs=u_codes[:, c * P : (c + 1) * P].bitcast(FP8X4),
+                        rhs_scale=u_scales[:, c * P : (c + 1) * P],
+                        start=True,
+                        stop=True,
+                    )
+                eng_copy = nc.vector.tensor_copy if c % 2 == 0 else nc.scalar.copy
+                eng_copy(
+                    out=gw[:, g, c * P : (c + 1) * P, :], in_=wt[:].rearrange("p t c -> p c t")
+                )
+
+        def quant_w(g):
+            nc.vector.quantize_mx(
+                out=w_codes[:, g * OUT : (g + 1) * OUT].bitcast(FP8X4),
+                scales=w_scales[:, g * OUT : (g + 1) * OUT],
+                in_=gw[:, g].rearrange("p n t -> p (n t)"),
+            )
+
+        gxs = {}
+        codes = {}
+
+        def transposes(i):
+            xw = xs[i][:].bitcast(F32)
+            gx = gpool.tile([P, SLOTS * IN], BF16, name="gx", tag="gx%d" % (i % NG), align_bytes=64)
+            g32 = gx[:].bitcast(F32).rearrange("p (s g r u) -> p s g r u", s=SLOTS, g=2, r=P, u=2)
+            banks = []
+            for s in range(SLOTS):
+                xt = psum.tile([P, 4, P], F32, name="xt", tag="xt%d" % s)
+                for a in range(4):
+                    w0 = s * 512 + a // 2 * 256
+                    nc.tensor.transpose(xt[:, a, :], xw[:, w0 + a % 2 : w0 + 256 : 2], ident_f[:])
+                banks.append(xt)
+            for s in range(SLOTS):
+                nc.scalar.copy(out=g32[:, s], in_=banks[s][:].rearrange("p (g u) r -> p g r u", u=2))
+            gxs[i] = gx
+            if i + RX < GROUPS:
+                load_x(i + RX, 1)
+
+        def quant_x(i, pieces):
+            xc = cpool.tile([P, SLOTS * 2 * P], U32, name="xc", tag="xc%d" % (i % NC), align_bytes=64)
+            xsc = cpool.tile([P, SLOTS * 2 * P], U8, name="xsc", tag="xsc%d" % (i % NC), align_bytes=64)
+            w = SLOTS * 2 * P // pieces
+            for h in range(pieces):
+                nc.vector.quantize_mx(
+                    out=xc[:, h * w : (h + 1) * w].bitcast(FP8X4),
+                    scales=xsc[:, h * w : (h + 1) * w],
+                    in_=gxs[i][:, 4 * h * w : 4 * (h + 1) * w],
+                )
+            codes[i] = (xc, xsc)
+
+        def multiply(i):
+            xc, xsc = codes[i]
+            ost = opool.tile([P, SLOTS * OUT], F32, name="ost", tag="ost%d" % (i % NO))
+            accs = []
+            for s in range(SLOTS):
+                acc = psum.tile([P, OUT], F32, name="acc", tag="acc%d" % s)
+                for g in range(2):
+                    c0 = (s * 2 + g) * P
+                    nc.tensor.matmul_mx(
+                        out=acc[:],
+                        lhsT=xc[:, c0 : c0 + P].bitcast(FP8X4),
+                        lhsT_scale=xsc[:, c0 : c0 + P],
+                        rhs=w_codes[:, g * OUT : (g + 1) * OUT].bitcast(FP8X4),
+                        rhs_scale=w_scales[:, g * OUT : (g + 1) * OUT],
+                        start=(g == 0),
+                        stop=(g == 1),
+                    )
+                accs.append(acc)
+            for s in range(SLOTS):
+                cols = slice(s * OUT, (s + 1) * OUT)
+                nc.vector.tensor_tensor(out=ost[:, cols], in0=accs[s][:], in1=bias_bc[:], op=ADD)
+                if i >= FINE:
+                    nc.sync.dma_start(out=og[i][:, cols], in_=ost[:, cols])
+            if i < FINE:
+                nc.gpsimd.dma_start(out=og[i], in_=ost[:])
+
+        transposes(0)
+        weight_half(0)
+        weight_half(1)
+        quant_w(0)
+        transposes(1)
+        quant_w(1)
+        quant_x(0, 4)
+        quant_x(1, 1)
+        for j in range(2, GROUPS + 2):
+            if j < GROUPS:
+                transposes(j)
+            multiply(j - 2)
+            if j < GROUPS:
+                quant_x(j, 1)

@@ -26,6 +26,9 @@ RX = 10
 NG = 3
 NC = 4
 NO = 4
+NP = 2
+DIRECT = 2
+VSLOTS = 1
 FINE = 13
 
 
@@ -42,6 +45,7 @@ def tile_sivalinear_t_kernel(
         gpool = ctx.enter_context(tc.tile_pool(name="gpool", bufs=1))
         cpool = ctx.enter_context(tc.tile_pool(name="cpool", bufs=1))
         opool = ctx.enter_context(tc.tile_pool(name="opool", bufs=1))
+        ppool = ctx.enter_context(tc.tile_pool(name="ppool", bufs=1))
         psum = ctx.enter_context(tc.psum_pool(name="psum", bufs=1))
         ctx.enter_context(tc.manual_schedule())
 
@@ -173,22 +177,39 @@ def tile_sivalinear_t_kernel(
 
         gxs = {}
         codes = {}
+        xps = {}
+
+        def reorder(i):
+            xp = ppool.tile([P, SLOTS * IN], BF16, name="xp", tag="xp%d" % (i % NP))
+            dst = xp[:].bitcast(F32).rearrange("p (b u r) -> p b u r", u=2, r=P)
+            src = xs[i][:].bitcast(F32).rearrange("p (b r u) -> p b u r", u=2, r=P)
+            c = 2 * VSLOTS
+            nc.vector.tensor_copy(out=dst[:, 0:c], in_=src[:, 0:c])
+            for s in range(VSLOTS, SLOTS):
+                nc.scalar.copy(out=dst[:, 2 * s : 2 * s + 2], in_=src[:, 2 * s : 2 * s + 2])
+            xps[i] = xp
+            if i + RX < GROUPS:
+                load_x(i + RX, 1)
+
+        def words(i, s, a):
+            base = s * 512 + a // 2 * 256
+            if i < DIRECT:
+                return xs[i][:].bitcast(F32)[:, base + a % 2 : base + 256 : 2]
+            return xps[i][:].bitcast(F32)[:, base + a % 2 * P : base + (a % 2 + 1) * P]
 
         def transposes(i):
-            xw = xs[i][:].bitcast(F32)
             gx = gpool.tile([P, SLOTS * IN], BF16, name="gx", tag="gx%d" % (i % NG), align_bytes=64)
             g32 = gx[:].bitcast(F32).rearrange("p (s g r u) -> p s g r u", s=SLOTS, g=2, r=P, u=2)
             banks = []
             for s in range(SLOTS):
                 xt = psum.tile([P, 4, P], F32, name="xt", tag="xt%d" % s)
                 for a in range(4):
-                    w0 = s * 512 + a // 2 * 256
-                    nc.tensor.transpose(xt[:, a, :], xw[:, w0 + a % 2 : w0 + 256 : 2], ident_f[:])
+                    nc.tensor.transpose(xt[:, a, :], words(i, s, a), ident_f[:])
                 banks.append(xt)
             for s in range(SLOTS):
                 nc.scalar.copy(out=g32[:, s], in_=banks[s][:].rearrange("p (g u) r -> p g r u", u=2))
             gxs[i] = gx
-            if i + RX < GROUPS:
+            if i < DIRECT and i + RX < GROUPS:
                 load_x(i + RX, 1)
 
         def quant_x(i, pieces):
@@ -236,10 +257,13 @@ def tile_sivalinear_t_kernel(
         transposes(1)
         quant_w(1)
         quant_x(0, 4)
+        reorder(2)
         quant_x(1, 1)
         for j in range(2, GROUPS + 2):
             if j < GROUPS:
                 transposes(j)
+            if j + 1 < GROUPS:
+                reorder(j + 1)
             multiply(j - 2)
             if j < GROUPS:
                 quant_x(j, 1)

@@ -22,10 +22,10 @@ SLOTS = 4
 GROUPS = TOKENS // (P * SLOTS)
 FLOPS = 2 * OUT * R * IN + 2 * TOKENS * IN * OUT
 
-RX = 10
+RX = 7
 NG = 3
 NC = 4
-NO = 4
+NO = 6
 NP = 2
 DIRECT = 2
 VSLOTS = 1
@@ -248,7 +248,7 @@ def tile_sivalinear_t_kernel(
                 if i >= FINE:
                     nc.sync.dma_start(out=og[i][:, cols], in_=ost[:, cols])
             if i < FINE:
-                nc.gpsimd.dma_start(out=og[i], in_=ost[:])
+                nc.sync.dma_start(out=og[i], in_=ost[:])
 
         transposes(0)
         weight_half(0)

@@ -26,9 +26,8 @@ RX = 7
 NG = 3
 NC = 4
 NO = 6
-NP = 2
+NP = 3
 DIRECT = 2
-VSLOTS = 1
 FINE = 13
 
 
@@ -183,10 +182,9 @@ def tile_sivalinear_t_kernel(
             xp = ppool.tile([P, SLOTS * IN], BF16, name="xp", tag="xp%d" % (i % NP))
             dst = xp[:].bitcast(F32).rearrange("p (b u r) -> p b u r", u=2, r=P)
             src = xs[i][:].bitcast(F32).rearrange("p (b r u) -> p b u r", u=2, r=P)
-            c = 2 * VSLOTS
-            nc.vector.tensor_copy(out=dst[:, 0:c], in_=src[:, 0:c])
-            for s in range(VSLOTS, SLOTS):
-                nc.scalar.copy(out=dst[:, 2 * s : 2 * s + 2], in_=src[:, 2 * s : 2 * s + 2])
+            nc.gpsimd.tensor_copy(out=dst[:, 0:2], in_=src[:, 0:2])
+            nc.scalar.copy(out=dst[:, 2:6], in_=src[:, 2:6])
+            nc.vector.tensor_copy(out=dst[:, 6:8], in_=src[:, 6:8])
             xps[i] = xp
             if i + RX < GROUPS:
                 load_x(i + RX, 1)
@@ -259,11 +257,12 @@ def tile_sivalinear_t_kernel(
         quant_x(0, 4)
         reorder(2)
         quant_x(1, 1)
+        reorder(3)
         for j in range(2, GROUPS + 2):
             if j < GROUPS:
                 transposes(j)
-            if j + 1 < GROUPS:
-                reorder(j + 1)
+            if j + 2 < GROUPS:
+                reorder(j + 2)
             multiply(j - 2)
             if j < GROUPS:
                 quant_x(j, 1)

@@ -27,7 +27,7 @@ NG = 3
 NC = 4
 NO = 6
 NP = 3
-DIRECT = 2
+DIRECT = 3
 FINE = 13
 
 
@@ -53,22 +53,24 @@ def tile_sivalinear_t_kernel(
         ident_f = const.tile([P, P], F32, name="ident_f")
         nc.vector.memset(rows[:].bitcast(I32), 0)
         nc.vector.memset(ones[:], 1.0)
+        warm = const.tile([P, 2], BF16, name="warm")
         masks.make_identity(nc, ident_f[:])
 
         s_col = const.tile([P, 4], BF16, name="s_col")
         u_sb = const.tile([P, 4 * R], BF16, name="u_sb")
         v_sb = const.tile([P, 4, IN], BF16, name="v_sb")
         u3 = u_sb[:].rearrange("p (o r) -> p o r", o=4)
-        nc.sync.dma_start(
-            out=s_col[:],
-            in_=siva_s.rearrange("(q j) -> q j", j=4),
-        )
         nc.sync.dma_start(out=u3[:, :, RT:R], in_=siva_u_d.rearrange("(o p) r -> p o r", p=P))
-        nc.sync.dma_start(out=u3[:, :, 0:RT], in_=siva_u_t.rearrange("(o p) r -> p o r", p=P))
+        nc.scalar.dma_start(out=s_col[:], in_=siva_s.rearrange("(q j) -> q j", j=4))
+        nc.scalar.dma_start(out=u3[:, :, 0:RT], in_=siva_u_t.rearrange("(o p) r -> p o r", p=P))
+        for q0, q1 in ((64, P), (32, 64), (16, 32)):
+            nc.sync.dma_start(
+                out=v_sb[q0:q1, :, :],
+                in_=siva_v_d[4 * q0 - RT : 4 * q1 - RT, :].rearrange("(q j) c -> q j c", j=4),
+            )
+        nc.scalar.dma_start(out=v_sb[0:16, :, :], in_=siva_v_t.rearrange("(q j) c -> q j c", j=4))
         nc.scalar.dma_start(out=rows[0:1, :], in_=bias.rearrange("(o n) -> o n", o=1))
-        qt = RT // 4
-        nc.sync.dma_start(out=v_sb[qt:P, :, :], in_=siva_v_d.rearrange("(q j) c -> q j c", j=4))
-        nc.sync.dma_start(out=v_sb[0:qt, :, :], in_=siva_v_t.rearrange("(q j) c -> q j c", j=4))
+        nc.scalar.copy(out=warm[:], in_=ones[:, 0:2])
 
         xs = {}
 
@@ -83,6 +85,57 @@ def tile_sivalinear_t_kernel(
         for i in range(1, RX):
             load_x(i, 1)
 
+        gxs = {}
+        codes = {}
+        xps = {}
+        banks = {}
+
+        def reorder(i):
+            xp = ppool.tile([P, SLOTS * IN], BF16, name="xp", tag="xp%d" % (i % NP))
+            dst = xp[:].bitcast(F32).rearrange("p (b u r) -> p b u r", u=2, r=P)
+            src = xs[i][:].bitcast(F32).rearrange("p (b r u) -> p b u r", u=2, r=P)
+            nc.gpsimd.tensor_copy(out=dst[:, 0:2], in_=src[:, 0:2])
+            nc.scalar.copy(out=dst[:, 2:6], in_=src[:, 2:6])
+            nc.vector.tensor_copy(out=dst[:, 6:8], in_=src[:, 6:8])
+            xps[i] = xp
+            if i + RX < GROUPS:
+                load_x(i + RX, 1)
+
+        def words(i, s, a):
+            base = s * 512 + a // 2 * 256
+            if i < DIRECT:
+                return xs[i][:].bitcast(F32)[:, base + a % 2 : base + 256 : 2]
+            return xps[i][:].bitcast(F32)[:, base + a % 2 * P : base + (a % 2 + 1) * P]
+
+        def transposes(i, slots, tags):
+            for s in slots:
+                xt = psum.tile([P, 4, P], F32, name="xt", tag="xt%d" % tags[s])
+                for a in range(4):
+                    nc.tensor.transpose(xt[:, a, :], words(i, s, a), ident_f[:])
+                banks[i, s] = xt
+
+        def empty(i, slots):
+            if i not in gxs:
+                gxs[i] = gpool.tile([P, SLOTS * IN], BF16, name="gx", tag="gx%d" % (i % NG), align_bytes=64)
+            g32 = gxs[i][:].bitcast(F32).rearrange("p (s g r u) -> p s g r u", s=SLOTS, g=2, r=P, u=2)
+            for s in slots:
+                nc.scalar.copy(out=g32[:, s], in_=banks[i, s][:].rearrange("p (g u) r -> p g r u", u=2))
+
+        def quant_x(i, h0, h1, pieces):
+            if i not in codes:
+                codes[i] = (
+                    cpool.tile([P, SLOTS * 2 * P], U32, name="xc", tag="xc%d" % (i % NC), align_bytes=64),
+                    cpool.tile([P, SLOTS * 2 * P], U8, name="xsc", tag="xsc%d" % (i % NC), align_bytes=64),
+                )
+            xc, xsc = codes[i]
+            w = SLOTS * 2 * P // pieces
+            for h in range(h0, h1):
+                nc.vector.quantize_mx(
+                    out=xc[:, h * w : (h + 1) * w].bitcast(FP8X4),
+                    scales=xsc[:, h * w : (h + 1) * w],
+                    in_=gxs[i][:, 4 * h * w : 4 * (h + 1) * w],
+                )
+
         gu = const.tile([P, OUT, 4], BF16, name="gu", align_bytes=64)
         uw = u_sb[:].bitcast(F32)
         s_b = s_col[:].rearrange("q (a e) -> q a e", a=2).unsqueeze(1).to_broadcast([P, P, 2, 2])
@@ -94,10 +147,9 @@ def tile_sivalinear_t_kernel(
                 nc.tensor.transpose(utb[:, k * P : (k + 1) * P], uw[:, w0 + k % 2 : w0 + 256 : 2], ident_f[:])
             utbs.append(utb)
 
-        ps_b = psum.tile([P, OUT], F32, name="ps_b", tag="acc2")
+        ps_b = psum.tile([P, OUT], F32, name="ps_b", tag="xt3")
         nc.tensor.matmul(out=ps_b[:], lhsT=ones[:], rhs=rows[:], start=True, stop=True)
         bias_bc = const.tile([P, OUT], F32, name="bias_bc")
-        nc.scalar.copy(out=bias_bc[:], in_=ps_b[:])
 
         for o in range(4):
             u16 = utbs[o // 2][:].bitcast(BF16).rearrange(
@@ -132,21 +184,10 @@ def tile_sivalinear_t_kernel(
                 in_=gv[:, g * 512 : (g + 1) * 512, :].rearrange("q c j -> q (c j)"),
             )
 
-        regroup_v(2, nc.scalar.copy)
-        regroup_v(3, nc.scalar.copy)
-        regroup_v(0, nc.vector.tensor_copy)
-        regroup_v(1, nc.vector.tensor_copy)
-        nc.vector.quantize_mx(
-            out=u_codes[:].bitcast(FP8X4),
-            scales=u_scales[:],
-            in_=gu[:].rearrange("p n t -> p (n t)"),
-        )
-        quant_v(0)
-        quant_v(1)
-
         gw = const.tile([P, 2, OUT, 4], BF16, name="gw", align_bytes=64)
         w_codes = const.tile([P, 2 * OUT], U32, name="w_codes", align_bytes=64)
         w_scales = const.tile([P, 2 * OUT], U8, name="w_scales", align_bytes=64)
+        wts = {}
 
         def weight_half(g):
             for c in range(4):
@@ -162,9 +203,13 @@ def tile_sivalinear_t_kernel(
                         start=True,
                         stop=True,
                     )
+                wts[g, c] = wt
+
+        def empty_w(g):
+            for c in range(4):
                 eng_copy = nc.vector.tensor_copy if c % 2 == 0 else nc.scalar.copy
                 eng_copy(
-                    out=gw[:, g, c * P : (c + 1) * P, :], in_=wt[:].rearrange("p t c -> p c t")
+                    out=gw[:, g, c * P : (c + 1) * P, :], in_=wts[g, c][:].rearrange("p t c -> p c t")
                 )
 
         def quant_w(g):
@@ -174,95 +219,76 @@ def tile_sivalinear_t_kernel(
                 in_=gw[:, g].rearrange("p n t -> p (n t)"),
             )
 
-        gxs = {}
-        codes = {}
-        xps = {}
+        accs = {}
 
-        def reorder(i):
-            xp = ppool.tile([P, SLOTS * IN], BF16, name="xp", tag="xp%d" % (i % NP))
-            dst = xp[:].bitcast(F32).rearrange("p (b u r) -> p b u r", u=2, r=P)
-            src = xs[i][:].bitcast(F32).rearrange("p (b r u) -> p b u r", u=2, r=P)
-            nc.gpsimd.tensor_copy(out=dst[:, 0:2], in_=src[:, 0:2])
-            nc.scalar.copy(out=dst[:, 2:6], in_=src[:, 2:6])
-            nc.vector.tensor_copy(out=dst[:, 6:8], in_=src[:, 6:8])
-            xps[i] = xp
-            if i + RX < GROUPS:
-                load_x(i + RX, 1)
-
-        def words(i, s, a):
-            base = s * 512 + a // 2 * 256
-            if i < DIRECT:
-                return xs[i][:].bitcast(F32)[:, base + a % 2 : base + 256 : 2]
-            return xps[i][:].bitcast(F32)[:, base + a % 2 * P : base + (a % 2 + 1) * P]
-
-        def transposes(i):
-            gx = gpool.tile([P, SLOTS * IN], BF16, name="gx", tag="gx%d" % (i % NG), align_bytes=64)
-            g32 = gx[:].bitcast(F32).rearrange("p (s g r u) -> p s g r u", s=SLOTS, g=2, r=P, u=2)
-            banks = []
-            for s in range(SLOTS):
-                xt = psum.tile([P, 4, P], F32, name="xt", tag="xt%d" % s)
-                for a in range(4):
-                    nc.tensor.transpose(xt[:, a, :], words(i, s, a), ident_f[:])
-                banks.append(xt)
-            for s in range(SLOTS):
-                nc.scalar.copy(out=g32[:, s], in_=banks[s][:].rearrange("p (g u) r -> p g r u", u=2))
-            gxs[i] = gx
-            if i < DIRECT and i + RX < GROUPS:
-                load_x(i + RX, 1)
-
-        def quant_x(i, pieces):
-            xc = cpool.tile([P, SLOTS * 2 * P], U32, name="xc", tag="xc%d" % (i % NC), align_bytes=64)
-            xsc = cpool.tile([P, SLOTS * 2 * P], U8, name="xsc", tag="xsc%d" % (i % NC), align_bytes=64)
-            w = SLOTS * 2 * P // pieces
-            for h in range(pieces):
-                nc.vector.quantize_mx(
-                    out=xc[:, h * w : (h + 1) * w].bitcast(FP8X4),
-                    scales=xsc[:, h * w : (h + 1) * w],
-                    in_=gxs[i][:, 4 * h * w : 4 * (h + 1) * w],
-                )
-            codes[i] = (xc, xsc)
-
-        def multiply(i):
+        def multiply(i, order):
             xc, xsc = codes[i]
-            ost = opool.tile([P, SLOTS * OUT], F32, name="ost", tag="ost%d" % (i % NO))
-            accs = []
-            for s in range(SLOTS):
-                acc = psum.tile([P, OUT], F32, name="acc", tag="acc%d" % s)
-                for g in range(2):
-                    c0 = (s * 2 + g) * P
-                    nc.tensor.matmul_mx(
-                        out=acc[:],
-                        lhsT=xc[:, c0 : c0 + P].bitcast(FP8X4),
-                        lhsT_scale=xsc[:, c0 : c0 + P],
-                        rhs=w_codes[:, g * OUT : (g + 1) * OUT].bitcast(FP8X4),
-                        rhs_scale=w_scales[:, g * OUT : (g + 1) * OUT],
-                        start=(g == 0),
-                        stop=(g == 1),
-                    )
-                accs.append(acc)
-            for s in range(SLOTS):
+            for s, g in order:
+                if g == 0:
+                    accs[i, s] = psum.tile([P, OUT], F32, name="acc", tag="acc%d" % s)
+                c0 = (s * 2 + g) * P
+                nc.tensor.matmul_mx(
+                    out=accs[i, s][:],
+                    lhsT=xc[:, c0 : c0 + P].bitcast(FP8X4),
+                    lhsT_scale=xsc[:, c0 : c0 + P],
+                    rhs=w_codes[:, g * OUT : (g + 1) * OUT].bitcast(FP8X4),
+                    rhs_scale=w_scales[:, g * OUT : (g + 1) * OUT],
+                    start=(g == 0),
+                    stop=(g == 1),
+                )
+
+        osts = {}
+
+        def finish(i, slots):
+            if i not in osts:
+                osts[i] = opool.tile([P, SLOTS * OUT], F32, name="ost", tag="ost%d" % (i % NO))
+            ost = osts[i]
+            for s in slots:
                 cols = slice(s * OUT, (s + 1) * OUT)
-                nc.vector.tensor_tensor(out=ost[:, cols], in0=accs[s][:], in1=bias_bc[:], op=ADD)
+                nc.vector.tensor_tensor(out=ost[:, cols], in0=accs[i, s][:], in1=bias_bc[:], op=ADD)
                 if i >= FINE:
                     nc.sync.dma_start(out=og[i][:, cols], in_=ost[:, cols])
-            if i < FINE:
-                nc.sync.dma_start(out=og[i], in_=ost[:])
+                elif s == SLOTS - 1:
+                    nc.sync.dma_start(out=og[i], in_=ost[:])
 
-        transposes(0)
+        nc.vector.quantize_mx(
+            out=u_codes[:].bitcast(FP8X4),
+            scales=u_scales[:],
+            in_=gu[:].rearrange("p n t -> p (n t)"),
+        )
+        regroup_v(0, nc.vector.tensor_copy)
+        regroup_v(1, nc.vector.tensor_copy)
+        quant_v(0)
+        regroup_v(2, nc.scalar.copy)
+        regroup_v(3, nc.scalar.copy)
+        transposes(0, (0, 1), (0, 1, 2, 0))
         weight_half(0)
+        empty(0, (0, 1))
+        quant_v(1)
+        empty_w(0)
+        transposes(0, (2, 3), (0, 1, 2, 0))
         weight_half(1)
+        quant_x(0, 0, 1, 2)
         quant_w(0)
-        transposes(1)
+        empty(0, (2, 3))
+        load_x(RX, 1)
+        empty_w(1)
+        nc.scalar.copy(out=bias_bc[:], in_=ps_b[:])
+        quant_x(0, 1, 2, 2)
         quant_w(1)
-        quant_x(0, 4)
-        reorder(2)
-        quant_x(1, 1)
-        reorder(3)
-        for j in range(2, GROUPS + 2):
+
+        by_slot = [(s, g) for s in range(SLOTS) for g in range(2)]
+        by_half = [(s, g) for g in range(2) for s in range(SLOTS)]
+        for j in range(1, GROUPS + 1):
             if j < GROUPS:
-                transposes(j)
-            if j + 2 < GROUPS:
+                transposes(j, range(SLOTS), range(SLOTS))
+                empty(j, range(SLOTS))
+                if j < DIRECT:
+                    load_x(j + RX, 1)
+            multiply(j - 1, by_half if j == 1 else by_slot)
+            finish(j - 1, (0, 1))
+            if j < GROUPS:
+                quant_x(j, 0, 1, 1)
+            if DIRECT <= j + 2 < GROUPS:
                 reorder(j + 2)
-            multiply(j - 2)
-            if j < GROUPS:
-                quant_x(j, 1)
+            finish(j - 1, (2, 3))

@@ -60,15 +60,15 @@ def tile_sivalinear_t_kernel(
         u_sb = const.tile([P, 4 * R], BF16, name="u_sb")
         v_sb = const.tile([P, 4, IN], BF16, name="v_sb")
         u3 = u_sb[:].rearrange("p (o r) -> p o r", o=4)
+        nc.sync.dma_start(out=u3[:, :, 0:RT], in_=siva_u_t.rearrange("(o p) r -> p o r", p=P))
         nc.sync.dma_start(out=u3[:, :, RT:R], in_=siva_u_d.rearrange("(o p) r -> p o r", p=P))
-        nc.scalar.dma_start(out=s_col[:], in_=siva_s.rearrange("(q j) -> q j", j=4))
-        nc.scalar.dma_start(out=u3[:, :, 0:RT], in_=siva_u_t.rearrange("(o p) r -> p o r", p=P))
+        nc.sync.dma_start(out=s_col[:], in_=siva_s.rearrange("(q j) -> q j", j=4))
         for q0, q1 in ((64, P), (32, 64), (16, 32)):
             nc.sync.dma_start(
                 out=v_sb[q0:q1, :, :],
                 in_=siva_v_d[4 * q0 - RT : 4 * q1 - RT, :].rearrange("(q j) c -> q j c", j=4),
             )
-        nc.scalar.dma_start(out=v_sb[0:16, :, :], in_=siva_v_t.rearrange("(q j) c -> q j c", j=4))
+        nc.sync.dma_start(out=v_sb[0:16, :, :], in_=siva_v_t.rearrange("(q j) c -> q j c", j=4))
         nc.scalar.dma_start(out=rows[0:1, :], in_=bias.rearrange("(o n) -> o n", o=1))
         nc.scalar.copy(out=warm[:], in_=ones[:, 0:2])
 
@@ -90,16 +90,12 @@ def tile_sivalinear_t_kernel(
         xps = {}
         banks = {}
 
-        def reorder(i):
-            xp = ppool.tile([P, SLOTS * IN], BF16, name="xp", tag="xp%d" % (i % NP))
-            dst = xp[:].bitcast(F32).rearrange("p (b u r) -> p b u r", u=2, r=P)
+        def reorder(i, eng_copy, s0, s1):
+            if i not in xps:
+                xps[i] = ppool.tile([P, SLOTS * IN], BF16, name="xp", tag="xp%d" % (i % NP))
+            dst = xps[i][:].bitcast(F32).rearrange("p (b u r) -> p b u r", u=2, r=P)
             src = xs[i][:].bitcast(F32).rearrange("p (b r u) -> p b u r", u=2, r=P)
-            nc.gpsimd.tensor_copy(out=dst[:, 0:2], in_=src[:, 0:2])
-            nc.scalar.copy(out=dst[:, 2:6], in_=src[:, 2:6])
-            nc.vector.tensor_copy(out=dst[:, 6:8], in_=src[:, 6:8])
-            xps[i] = xp
-            if i + RX < GROUPS:
-                load_x(i + RX, 1)
+            eng_copy(out=dst[:, 2 * s0 : 2 * s1], in_=src[:, 2 * s0 : 2 * s1])
 
         def words(i, s, a):
             base = s * 512 + a // 2 * 256
@@ -278,17 +274,34 @@ def tile_sivalinear_t_kernel(
         quant_w(1)
 
         by_slot = [(s, g) for s in range(SLOTS) for g in range(2)]
-        by_half = [(s, g) for g in range(2) for s in range(SLOTS)]
-        for j in range(1, GROUPS + 1):
-            if j < GROUPS:
-                transposes(j, range(SLOTS), range(SLOTS))
-                empty(j, range(SLOTS))
-                if j < DIRECT:
-                    load_x(j + RX, 1)
-            multiply(j - 1, by_half if j == 1 else by_slot)
-            finish(j - 1, (0, 1))
-            if j < GROUPS:
-                quant_x(j, 0, 1, 1)
-            if DIRECT <= j + 2 < GROUPS:
-                reorder(j + 2)
-            finish(j - 1, (2, 3))
+        transposes(1, range(SLOTS), range(SLOTS))
+        empty(1, range(SLOTS))
+        load_x(1 + RX, 1)
+        reorder(3, nc.gpsimd.tensor_copy, 0, 2)
+        for j in range(2, GROUPS + 2):
+            for h, slots in enumerate(((0, 1), (2, 3))):
+                passes = by_slot[4 * h : 4 * h + 4]
+                if j == 2:
+                    multiply(j - 2, passes)
+                if j < GROUPS:
+                    transposes(j, slots, range(SLOTS))
+                    empty(j, slots)
+                if j > 2:
+                    multiply(j - 2, passes)
+                finish(j - 2, slots)
+                if j == 2 and h == 0:
+                    quant_x(1, 0, 1, 1)
+                    reorder(3, nc.vector.tensor_copy, 2, 4)
+                    load_x(3 + RX, 1)
+                if j < GROUPS:
+                    quant_x(j, h, h + 1, 2)
+                if DIRECT <= j + 2 < GROUPS:
+                    if h == 0:
+                        reorder(j + 2, nc.gpsimd.tensor_copy, 0, 1)
+                        reorder(j + 2, nc.vector.tensor_copy, 3, 4)
+                    else:
+                        reorder(j + 2, nc.scalar.copy, 1, 3)
+                        if j + 2 + RX < GROUPS:
+                            load_x(j + 2 + RX, 1)
+            if j < DIRECT:
+                load_x(j + RX, 1)

@@ -63,12 +63,9 @@ def tile_sivalinear_t_kernel(
         nc.sync.dma_start(out=u3[:, :, 0:RT], in_=siva_u_t.rearrange("(o p) r -> p o r", p=P))
         nc.sync.dma_start(out=u3[:, :, RT:R], in_=siva_u_d.rearrange("(o p) r -> p o r", p=P))
         nc.sync.dma_start(out=s_col[:], in_=siva_s.rearrange("(q j) -> q j", j=4))
-        for q0, q1 in ((64, P), (32, 64), (16, 32)):
-            nc.sync.dma_start(
-                out=v_sb[q0:q1, :, :],
-                in_=siva_v_d[4 * q0 - RT : 4 * q1 - RT, :].rearrange("(q j) c -> q j c", j=4),
-            )
-        nc.sync.dma_start(out=v_sb[0:16, :, :], in_=siva_v_t.rearrange("(q j) c -> q j c", j=4))
+        qt = RT // 4
+        nc.sync.dma_start(out=v_sb[qt:P, :, :], in_=siva_v_d.rearrange("(q j) c -> q j c", j=4))
+        nc.sync.dma_start(out=v_sb[0:qt, :, :], in_=siva_v_t.rearrange("(q j) c -> q j c", j=4))
         nc.scalar.dma_start(out=rows[0:1, :], in_=bias.rearrange("(o n) -> o n", o=1))
         nc.scalar.copy(out=warm[:], in_=ones[:, 0:2])
 

@@ -28,6 +28,7 @@ NC = 4
 NO = 6
 NP = 3
 DIRECT = 3
+RUN = 3
 FINE = 13
 
 
@@ -252,53 +253,72 @@ def tile_sivalinear_t_kernel(
         regroup_v(0, nc.vector.tensor_copy)
         regroup_v(1, nc.vector.tensor_copy)
         quant_v(0)
+        nc.scalar.copy(out=bias_bc[:], in_=ps_b[:])
         regroup_v(2, nc.scalar.copy)
         regroup_v(3, nc.scalar.copy)
-        transposes(0, (0, 1), (0, 1, 2, 0))
+        transposes(0, (0, 1), range(SLOTS))
         weight_half(0)
         empty(0, (0, 1))
         quant_v(1)
         empty_w(0)
-        transposes(0, (2, 3), (0, 1, 2, 0))
+        transposes(0, (2, 3), range(SLOTS))
         weight_half(1)
         quant_x(0, 0, 1, 2)
         quant_w(0)
         empty(0, (2, 3))
         load_x(RX, 1)
         empty_w(1)
-        nc.scalar.copy(out=bias_bc[:], in_=ps_b[:])
         quant_x(0, 1, 2, 2)
         quant_w(1)
 
-        by_slot = [(s, g) for s in range(SLOTS) for g in range(2)]
         transposes(1, range(SLOTS), range(SLOTS))
         empty(1, range(SLOTS))
         load_x(1 + RX, 1)
         reorder(3, nc.gpsimd.tensor_copy, 0, 2)
-        for j in range(2, GROUPS + 2):
-            for h, slots in enumerate(((0, 1), (2, 3))):
-                passes = by_slot[4 * h : 4 * h + 4]
-                if j == 2:
-                    multiply(j - 2, passes)
-                if j < GROUPS:
-                    transposes(j, slots, range(SLOTS))
-                    empty(j, slots)
-                if j > 2:
-                    multiply(j - 2, passes)
-                finish(j - 2, slots)
-                if j == 2 and h == 0:
-                    quant_x(1, 0, 1, 1)
-                    reorder(3, nc.vector.tensor_copy, 2, 4)
-                    load_x(3 + RX, 1)
-                if j < GROUPS:
-                    quant_x(j, h, h + 1, 2)
-                if DIRECT <= j + 2 < GROUPS:
-                    if h == 0:
-                        reorder(j + 2, nc.gpsimd.tensor_copy, 0, 1)
-                        reorder(j + 2, nc.vector.tensor_copy, 3, 4)
-                    else:
-                        reorder(j + 2, nc.scalar.copy, 1, 3)
-                        if j + 2 + RX < GROUPS:
-                            load_x(j + 2 + RX, 1)
-            if j < DIRECT:
-                load_x(j + RX, 1)
+        reorder(3, nc.vector.tensor_copy, 2, 4)
+        load_x(3 + RX, 1)
+        total = GROUPS * SLOTS
+        head = 2 * SLOTS
+
+        def run_slots(first):
+            return [divmod(n, SLOTS) for n in range(first, min(first + RUN, total))]
+
+        def reorder_steady(i):
+            if i < GROUPS:
+                reorder(i, nc.gpsimd.tensor_copy, 0, 1)
+                reorder(i, nc.gpsimd.tensor_copy, 3, 4)
+                reorder(i, nc.scalar.copy, 1, 3)
+                if i + RX < GROUPS:
+                    load_x(i + RX, 1)
+
+        def transpose_run(r):
+            for i, s in run_slots(head + RUN * r):
+                transposes(i, (s,), range(SLOTS))
+                empty(i, (s,))
+            for i, s in run_slots(head + RUN * r):
+                if s == SLOTS - 1:
+                    if i < DIRECT:
+                        load_x(i + RX, 1)
+                    reorder_steady(i + NP)
+
+        def multiply_run(r):
+            for i, s in run_slots(RUN * r):
+                multiply(i, ((s, 0), (s, 1)))
+
+        def finish_run(r, quantised):
+            for i, s in run_slots(RUN * r):
+                finish(i, (s,))
+            for i, s in quantised:
+                if s % 2 == 1:
+                    quant_x(i, s // 2, s // 2 + 1, 2)
+
+        multiply_run(0)
+        transpose_run(0)
+        reorder_steady(4)
+        finish_run(0, [(1, 1), (1, 3)])
+        transpose_run(1)
+        for r in range(1, -(-total // RUN)):
+            multiply_run(r)
+            transpose_run(r + 1)
+            first = run_slots(head) if r == 1 else []
+            finish_run(r, first + run_slots(head + RUN * r))

from contextlib import ExitStack

import concourse.masks as masks
import concourse.mybir as mybir

BF16 = mybir.dt.bfloat16
F32 = mybir.dt.float32
I32 = mybir.dt.int32
U32 = mybir.dt.uint32
U8 = mybir.dt.uint8
FP8X4 = mybir.dt.float8_e4m3fn_x4
ADD = mybir.AluOpType.add
MULT = mybir.AluOpType.mult

P = 128
TOKENS = 8192
IN = 1024
OUT = 512
R = 512
RT = 64
SLOTS = 4
GROUPS = TOKENS // (P * SLOTS)
FLOPS = 2 * OUT * R * IN + 2 * TOKENS * IN * OUT

RX = 7
NG = 3
NC = 4
NO = 6
NP = 3
DIRECT = 3
RUN = 3
FINE = 13


def tile_sivalinear_t_kernel(
    tc, x, siva_u_t, siva_u_d, siva_s, siva_v_t, siva_v_d, bias, out
):
    nc = tc.nc
    xg = x.flatten_outer_dims().rearrange("(i p s) k -> i p (s k)", p=P, s=SLOTS)
    og = out.flatten_outer_dims().rearrange("(i p s) n -> i p (s n)", p=P, s=SLOTS)

    with ExitStack() as ctx:
        const = ctx.enter_context(tc.tile_pool(name="const", bufs=1))
        xpool = ctx.enter_context(tc.tile_pool(name="xpool", bufs=1))
        gpool = ctx.enter_context(tc.tile_pool(name="gpool", bufs=1))
        cpool = ctx.enter_context(tc.tile_pool(name="cpool", bufs=1))
        opool = ctx.enter_context(tc.tile_pool(name="opool", bufs=1))
        ppool = ctx.enter_context(tc.tile_pool(name="ppool", bufs=1))
        psum = ctx.enter_context(tc.psum_pool(name="psum", bufs=1))
        ctx.enter_context(tc.manual_schedule())

        rows = const.tile([P, OUT], BF16, name="rows")
        ones = const.tile([P, P], BF16, name="ones")
        ident_f = const.tile([P, P], F32, name="ident_f")
        nc.vector.memset(rows[:].bitcast(I32), 0)
        nc.vector.memset(ones[:], 1.0)
        warm = const.tile([P, 2], BF16, name="warm")
        masks.make_identity(nc, ident_f[:])

        s_col = const.tile([P, 4], BF16, name="s_col")
        u_sb = const.tile([P, 4 * R], BF16, name="u_sb")
        v_sb = const.tile([P, 4, IN], BF16, name="v_sb")
        u3 = u_sb[:].rearrange("p (o r) -> p o r", o=4)
        nc.sync.dma_start(out=u3[:, :, 0:RT], in_=siva_u_t.rearrange("(o p) r -> p o r", p=P))
        nc.sync.dma_start(out=u3[:, :, RT:R], in_=siva_u_d.rearrange("(o p) r -> p o r", p=P))
        nc.sync.dma_start(out=s_col[:], in_=siva_s.rearrange("(q j) -> q j", j=4))
        qt = RT // 4
        nc.sync.dma_start(out=v_sb[qt:P, :, :], in_=siva_v_d.rearrange("(q j) c -> q j c", j=4))
        nc.sync.dma_start(out=v_sb[0:qt, :, :], in_=siva_v_t.rearrange("(q j) c -> q j c", j=4))
        nc.scalar.dma_start(out=rows[0:1, :], in_=bias.rearrange("(o n) -> o n", o=1))
        nc.scalar.copy(out=warm[:], in_=ones[:, 0:2])

        xs = {}

        def load_x(i, pieces):
            t = xpool.tile([P, SLOTS * IN], BF16, name="xs", tag="xs%d" % (i % RX))
            w = SLOTS * IN // pieces
            for h in range(pieces):
                nc.sync.dma_start(out=t[:, h * w : (h + 1) * w], in_=xg[i][:, h * w : (h + 1) * w])
            xs[i] = t

        load_x(0, 2)
        for i in range(1, RX):
            load_x(i, 1)

        gxs = {}
        codes = {}
        xps = {}
        banks = {}

        def reorder(i, eng_copy, s0, s1):
            if i not in xps:
                xps[i] = ppool.tile([P, SLOTS * IN], BF16, name="xp", tag="xp%d" % (i % NP))
            dst = xps[i][:].bitcast(F32).rearrange("p (b u r) -> p b u r", u=2, r=P)
            src = xs[i][:].bitcast(F32).rearrange("p (b r u) -> p b u r", u=2, r=P)
            eng_copy(out=dst[:, 2 * s0 : 2 * s1], in_=src[:, 2 * s0 : 2 * s1])

        def words(i, s, a):
            base = s * 512 + a // 2 * 256
            if i < DIRECT:
                return xs[i][:].bitcast(F32)[:, base + a % 2 : base + 256 : 2]
            return xps[i][:].bitcast(F32)[:, base + a % 2 * P : base + (a % 2 + 1) * P]

        def transposes(i, slots, tags):
            for s in slots:
                xt = psum.tile([P, 4, P], F32, name="xt", tag="xt%d" % tags[s])
                for a in range(4):
                    nc.tensor.transpose(xt[:, a, :], words(i, s, a), ident_f[:])
                banks[i, s] = xt

        def empty(i, slots):
            if i not in gxs:
                gxs[i] = gpool.tile([P, SLOTS * IN], BF16, name="gx", tag="gx%d" % (i % NG), align_bytes=64)
            g32 = gxs[i][:].bitcast(F32).rearrange("p (s g r u) -> p s g r u", s=SLOTS, g=2, r=P, u=2)
            for s in slots:
                nc.scalar.copy(out=g32[:, s], in_=banks[i, s][:].rearrange("p (g u) r -> p g r u", u=2))

        def quant_x(i, h0, h1, pieces):
            if i not in codes:
                codes[i] = (
                    cpool.tile([P, SLOTS * 2 * P], U32, name="xc", tag="xc%d" % (i % NC), align_bytes=64),
                    cpool.tile([P, SLOTS * 2 * P], U8, name="xsc", tag="xsc%d" % (i % NC), align_bytes=64),
                )
            xc, xsc = codes[i]
            w = SLOTS * 2 * P // pieces
            for h in range(h0, h1):
                nc.vector.quantize_mx(
                    out=xc[:, h * w : (h + 1) * w].bitcast(FP8X4),
                    scales=xsc[:, h * w : (h + 1) * w],
                    in_=gxs[i][:, 4 * h * w : 4 * (h + 1) * w],
                )

        gu = const.tile([P, OUT, 4], BF16, name="gu", align_bytes=64)
        uw = u_sb[:].bitcast(F32)
        s_b = s_col[:].rearrange("q (a e) -> q a e", a=2).unsqueeze(1).to_broadcast([P, P, 2, 2])
        utbs = []
        for b in range(2):
            utb = psum.tile([P, 4 * P], F32, name="utb", tag="acc%d" % b)
            for k in range(4):
                w0 = (2 * b + k // 2) * 256
                nc.tensor.transpose(utb[:, k * P : (k + 1) * P], uw[:, w0 + k % 2 : w0 + 256 : 2], ident_f[:])
            utbs.append(utb)

        ps_b = psum.tile([P, OUT], F32, name="ps_b", tag="xt3")
        nc.tensor.matmul(out=ps_b[:], lhsT=ones[:], rhs=rows[:], start=True, stop=True)
        bias_bc = const.tile([P, OUT], F32, name="bias_bc")

        for o in range(4):
            u16 = utbs[o // 2][:].bitcast(BF16).rearrange(
                "p (o a n e) -> p o a n e", o=2, a=2, n=P, e=2
            )
            nc.vector.tensor_tensor(
                out=gu[:, o * P : (o + 1) * P, :].rearrange("p n (a e) -> p n a e", a=2),
                in0=u16[:, o % 2].rearrange("p a n e -> p n a e"),
                in1=s_b,
                op=MULT,
            )

        gv = const.tile([P, IN, 4], BF16, name="gv", align_bytes=64)

        def regroup_v(a, eng_copy):
            eng_copy(
                out=gv[:, a * 256 : (a + 1) * 256, :].rearrange("q (e p) j -> q e p j", e=2),
                in_=v_sb[:, :, a // 2 * 512 : (a // 2 + 1) * 512].rearrange("q j (p t) -> q t p j", t=4)[
                    :, a % 2 * 2 : a % 2 * 2 + 2
                ],
            )

        u_codes = const.tile([P, OUT], U32, name="u_codes", align_bytes=64)
        u_scales = const.tile([P, OUT], U8, name="u_scales", align_bytes=64)
        v_codes = const.tile([P, IN], U32, name="v_codes", align_bytes=64)
        v_scales = const.tile([P, IN], U8, name="v_scales", align_bytes=64)

        def quant_v(g):
            nc.vector.quantize_mx(
                out=v_codes[:, g * 512 : (g + 1) * 512].bitcast(FP8X4),
                scales=v_scales[:, g * 512 : (g + 1) * 512],
                in_=gv[:, g * 512 : (g + 1) * 512, :].rearrange("q c j -> q (c j)"),
            )

        gw = const.tile([P, 2, OUT, 4], BF16, name="gw", align_bytes=64)
        w_codes = const.tile([P, 2 * OUT], U32, name="w_codes", align_bytes=64)
        w_scales = const.tile([P, 2 * OUT], U8, name="w_scales", align_bytes=64)
        wts = {}

        def weight_half(g):
            for c in range(4):
                wt = psum.tile([P, 4, P], F32, name="wt", tag="acc%d" % c)
                for t in range(4):
                    m = (4 * g + t) * P
                    nc.tensor.matmul_mx(
                        out=wt[:, t, :],
                        lhsT=v_codes[:, m : m + P].bitcast(FP8X4),
                        lhsT_scale=v_scales[:, m : m + P],
                        rhs=u_codes[:, c * P : (c + 1) * P].bitcast(FP8X4),
                        rhs_scale=u_scales[:, c * P : (c + 1) * P],
                        start=True,
                        stop=True,
                    )
                wts[g, c] = wt

        def empty_w(g):
            for c in range(4):
                eng_copy = nc.vector.tensor_copy if c % 2 == 0 else nc.scalar.copy
                eng_copy(
                    out=gw[:, g, c * P : (c + 1) * P, :], in_=wts[g, c][:].rearrange("p t c -> p c t")
                )

        def quant_w(g):
            nc.vector.quantize_mx(
                out=w_codes[:, g * OUT : (g + 1) * OUT].bitcast(FP8X4),
                scales=w_scales[:, g * OUT : (g + 1) * OUT],
                in_=gw[:, g].rearrange("p n t -> p (n t)"),
            )

        accs = {}

        def multiply(i, order):
            xc, xsc = codes[i]
            for s, g in order:
                if g == 0:
                    accs[i, s] = psum.tile([P, OUT], F32, name="acc", tag="acc%d" % s)
                c0 = (s * 2 + g) * P
                nc.tensor.matmul_mx(
                    out=accs[i, s][:],
                    lhsT=xc[:, c0 : c0 + P].bitcast(FP8X4),
                    lhsT_scale=xsc[:, c0 : c0 + P],
                    rhs=w_codes[:, g * OUT : (g + 1) * OUT].bitcast(FP8X4),
                    rhs_scale=w_scales[:, g * OUT : (g + 1) * OUT],
                    start=(g == 0),
                    stop=(g == 1),
                )

        osts = {}

        def finish(i, slots):
            if i not in osts:
                osts[i] = opool.tile([P, SLOTS * OUT], F32, name="ost", tag="ost%d" % (i % NO))
            ost = osts[i]
            for s in slots:
                cols = slice(s * OUT, (s + 1) * OUT)
                nc.vector.tensor_tensor(out=ost[:, cols], in0=accs[i, s][:], in1=bias_bc[:], op=ADD)
                if i >= FINE:
                    nc.sync.dma_start(out=og[i][:, cols], in_=ost[:, cols])
                elif s == SLOTS - 1:
                    nc.sync.dma_start(out=og[i], in_=ost[:])

        nc.vector.quantize_mx(
            out=u_codes[:].bitcast(FP8X4),
            scales=u_scales[:],
            in_=gu[:].rearrange("p n t -> p (n t)"),
        )
        regroup_v(0, nc.vector.tensor_copy)
        regroup_v(1, nc.vector.tensor_copy)
        quant_v(0)
        nc.scalar.copy(out=bias_bc[:], in_=ps_b[:])
        regroup_v(2, nc.scalar.copy)
        regroup_v(3, nc.scalar.copy)
        transposes(0, (0, 1), range(SLOTS))
        weight_half(0)
        empty(0, (0, 1))
        quant_v(1)
        empty_w(0)
        transposes(0, (2, 3), range(SLOTS))
        weight_half(1)
        quant_x(0, 0, 1, 2)
        quant_w(0)
        empty(0, (2, 3))
        load_x(RX, 1)
        empty_w(1)
        quant_x(0, 1, 2, 2)
        quant_w(1)

        transposes(1, range(SLOTS), range(SLOTS))
        empty(1, range(SLOTS))
        load_x(1 + RX, 1)
        reorder(3, nc.gpsimd.tensor_copy, 0, 2)
        reorder(3, nc.vector.tensor_copy, 2, 4)
        load_x(3 + RX, 1)
        total = GROUPS * SLOTS
        head = 2 * SLOTS

        def run_slots(first):
            return [divmod(n, SLOTS) for n in range(first, min(first + RUN, total))]

        def reorder_steady(i):
            if i < GROUPS:
                reorder(i, nc.gpsimd.tensor_copy, 0, 1)
                reorder(i, nc.gpsimd.tensor_copy, 3, 4)
                reorder(i, nc.scalar.copy, 1, 3)
                if i + RX < GROUPS:
                    load_x(i + RX, 1)

        def transpose_run(r):
            for i, s in run_slots(head + RUN * r):
                transposes(i, (s,), range(SLOTS))
                empty(i, (s,))
            for i, s in run_slots(head + RUN * r):
                if s == SLOTS - 1:
                    if i < DIRECT:
                        load_x(i + RX, 1)
                    reorder_steady(i + NP)

        def multiply_run(r):
            for i, s in run_slots(RUN * r):
                multiply(i, ((s, 0), (s, 1)))

        def finish_run(r, quantised):
            for i, s in run_slots(RUN * r):
                finish(i, (s,))
            for i, s in quantised:
                if s % 2 == 1:
                    quant_x(i, s // 2, s // 2 + 1, 2)

        multiply_run(0)
        transpose_run(0)
        reorder_steady(4)
        finish_run(0, [(1, 1), (1, 3)])
        transpose_run(1)
        for r in range(1, -(-total // RUN)):
            multiply_run(r)
            transpose_run(r + 1)
            first = run_slots(head) if r == 1 else []
            finish_run(r, first + run_slots(head + RUN * r))
